import numpy as np
import ml_dtypes


def mxq(x, axis, fmt="e4m3"):
    dtype, down = {"e4m3": (ml_dtypes.float8_e4m3fn, 7), "e5m2": (ml_dtypes.float8_e5m2, 14)}[fmt]
    v = np.moveaxis(np.asarray(x, np.float32).astype(ml_dtypes.bfloat16).astype(np.float64), axis, -1)
    blocks = v.reshape(v.shape[:-1] + (-1, 32))
    amax = np.abs(blocks).max(-1, keepdims=True)
    byte = np.maximum(np.where(amax > 0, np.frexp(amax)[1] - 1 + 127, 0) - down, 1)
    scale = np.exp2(byte - 127.0)
    codes = (blocks / scale).astype(np.float32).astype(dtype).astype(np.float64)
    return np.moveaxis((codes * scale).reshape(v.shape), -1, axis)


WIDE = False


def mx_kscale(k):
    if not WIDE:
        return np.ones(k)
    levels = np.array([10, -10, 5, -5, 0])
    a = np.random.permutation(np.resize(levels, k // 512 * 4)).reshape(k // 512, 4)
    idx = np.arange(k)
    return np.exp2(a[idx // 512, idx % 128 // 32])


BF16 = ml_dtypes.bfloat16


def bf(x):
    return np.asarray(x, np.float32).astype(BF16)


def f64(x):
    return np.asarray(x).astype(np.float64)


B, NSEG, SEGLEN, HEADS, D, E, I = 1, 4, 64, 2, 512, 2, 8192
S = NSEG * SEGLEN
HID = HEADS * D
NPREV = NSEG - 1


def softmax(v):
    e = np.exp(v - v.max(-1, keepdims=True))
    return e / e.sum(-1, keepdims=True)


def merge(w, ew):
    m = 0.0
    for e in range(E):
        m = m + ew[..., e, None, None] * w[e]
    return m


def setup_inputs():
    s, t = mx_kscale(D), mx_kscale(I)
    return {'x_mh': bf(np.random.standard_normal((B, S, HID)) * np.tile(s, HEADS)),
            'ew': bf(softmax(1.5 * np.random.standard_normal((B, NPREV, HEADS, E)))),
            'first_linear': bf(np.random.standard_normal((E, I, D)) * 2.0 / np.sqrt(D) * t[:, None] / s),
            'second_linear': bf(np.random.standard_normal((E, D, I)) * 2.0 / np.sqrt(I) / t)}


def reference(x_mh, ew, first_linear, second_linear):
    w = f64(ew)
    m1q = mxq(merge(f64(first_linear), w), 4, 'e4m3')
    m2q = mxq(merge(f64(second_linear), w), 4, 'e4m3')
    xr = f64(x_mh).reshape(B, NSEG, SEGLEN, HEADS, D).reshape(B, NSEG, HEADS, SEGLEN, D)
    xq = mxq(xr, 4, 'e4m3')
    h = np.maximum(xq[:, 1:] @ m1q.swapaxes(-1, -2), 0.0)
    res = mxq(h, 4, 'e4m3') @ m2q.swapaxes(-1, -2)
    h0 = np.maximum(xq[:, 0] @ m1q[:, 0].swapaxes(-1, -2), 0.0)
    r0 = mxq(h0, 3, 'e4m3') @ m2q[:, 0].swapaxes(-1, -2)
    out = np.concatenate([r0[:, None], res], axis=1)
    return out.reshape(B, S, HEADS, D).reshape(B, S, HID)

@@ -1,0 +1,290 @@
+from contextlib import ExitStack
+
+import concourse.mybir as mybir
+from concourse.masks import make_identity
+
+BF16 = mybir.dt.bfloat16
+F32 = mybir.dt.float32
+I32 = mybir.dt.int32
+U32 = mybir.dt.uint32
+U8 = mybir.dt.uint8
+FP8X4 = mybir.dt.float8_e4m3fn_x4
+MULT = mybir.AluOpType.mult
+ADD = mybir.AluOpType.add
+COPY = mybir.ActivationFunctionType.Copy
+RELU = mybir.ActivationFunctionType.Relu
+
+P = 128
+PACK = 4
+K_PASS = P * PACK
+EXPERTS = 2
+GROUPS = 2
+GROUP_ROWS = 64
+FEATURES = 512
+HIDDEN = 8192
+UNITS = HIDDEN // K_PASS
+PAIRS = 6
+BANK_WORDS = 512
+BANK_VALUES = 2 * BANK_WORDS
+BANKS_PER_UNIT = 2
+UNIT_VALUES = BANKS_PER_UNIT * BANK_VALUES
+UNIT_WORDS = UNIT_VALUES // PACK
+CHUNK_UNITS = 2
+CHUNK_VALUES = EXPERTS * CHUNK_UNITS * UNIT_VALUES
+
+FLOPS = 2 * 2 * 512 * FEATURES * HIDDEN
+
+
+def tile_mh_lori_pa_k_kernel(tc, x_mh, ew, first_linear, second_linear, out):
+    nc = tc.nc
+    x_rows = x_mh.rearrange("b s (h d) -> (b s h) d", d=FEATURES)
+    out_rows = out.rearrange("b s (h d) -> (b s h) d", d=FEATURES)
+
+    with ExitStack() as ctx:
+        const = ctx.enter_context(tc.tile_pool(name="const", bufs=1))
+        natural = ctx.enter_context(tc.tile_pool(name="natural", bufs=2))
+        work = ctx.enter_context(tc.tile_pool(name="work", bufs=2))
+        raw_psum = ctx.enter_context(tc.psum_pool(name="raw_psum", bufs=2))
+
+        identity = const.tile([P, P], F32)
+        make_identity(nc, identity[:])
+
+        ew_bf16 = const.tile([P, PAIRS * EXPERTS], BF16)
+        nc.sync.dma_start(
+            out=ew_bf16[:], in_=ew.rearrange("b n g e -> (b n g e)").partition_broadcast(P)
+        )
+        ew_f32 = const.tile([P, PAIRS * EXPERTS], F32)
+        nc.vector.tensor_copy(out=ew_f32[:], in_=ew_bf16[:])
+
+        def mixing_weight(pair, expert):
+            column = EXPERTS * pair + expert
+            return ew_f32[:, column : column + 1]
+
+        h_codes = const.tile([P, PAIRS * UNITS * P], U32, align_bytes=64)
+        h_scales = const.tile([P, PAIRS * UNITS * P], U8, align_bytes=64)
+
+        def token_columns(pair):
+            if pair < GROUPS:
+                return 0, P
+            group = pair % GROUPS
+            return group * GROUP_ROWS, (group + 1) * GROUP_ROWS
+
+        def token_block(pair):
+            weight_segment, group = divmod(pair, GROUPS)
+            return group if weight_segment == 0 else weight_segment + 1
+
+        for pair in range(GROUPS, PAIRS):
+            zero_low = GROUP_ROWS - token_columns(pair)[0]
+            pair_words = slice(pair * UNITS * P, (pair + 1) * UNITS * P)
+            nc.vector.memset(
+                h_codes[:, pair_words]
+                .bitcast(I32)
+                .rearrange("p (n k) -> p n k", k=P)[:, :, zero_low : zero_low + GROUP_ROWS],
+                0,
+            )
+            nc.vector.memset(
+                h_scales[:, pair_words]
+                .bitcast(I32)
+                .rearrange("p (n k) -> p n k", k=P // 4)[
+                    :, :, zero_low // 4 : (zero_low + GROUP_ROWS) // 4
+                ],
+                0,
+            )
+
+        def transposed_bank(block_of, tag):
+            bank = raw_psum.tile([P, BANK_WORDS], F32, name=tag, tag=tag)
+            for u in range(2):
+                for r in range(2):
+                    first = (2 * u + r) * P
+                    nc.tensor.transpose(bank[:, first : first + P], block_of(u, r), identity[:])
+            return bank[:].bitcast(BF16).rearrange("p (u c) -> p c u", u=2)
+
+        def by_plane(flat):
+            return flat.rearrange("p (c u) -> p c u", u=2)
+
+        x_natural = const.tile([P, 4 * FEATURES], BF16)
+        x_blocks = x_natural[:].rearrange("p (k d) -> p k d", d=FEATURES)
+        for segment in range(2):
+            nc.sync.dma_start(
+                out=x_blocks[segment * GROUP_ROWS : (segment + 1) * GROUP_ROWS, 0:2, :],
+                in_=x_rows[segment * P : (segment + 1) * P, :].rearrange(
+                    "(g j) d -> j g d", g=GROUPS
+                ),
+            )
+        nc.sync.dma_start(
+            out=x_blocks[:, 2:4, :],
+            in_=x_rows[2 * P : 4 * P, :].rearrange("(k p) d -> p k d", p=P),
+        )
+        x_words = x_natural[:].bitcast(F32).rearrange("p (k q) -> p k q", q=FEATURES // 2)
+        x_grouped = const.tile([P, UNIT_VALUES], BF16, align_bytes=64)
+        for j in range(BANKS_PER_UNIT):
+            bank = transposed_bank(
+                lambda u, r, j=j: x_words[:, 2 * j + r, u * P : (u + 1) * P], "raw0"
+            )
+            nc.vector.tensor_copy(
+                out=by_plane(x_grouped[:, j * BANK_VALUES : (j + 1) * BANK_VALUES]), in_=bank
+            )
+        x_codes = const.tile([P, UNIT_WORDS], U32, align_bytes=64)
+        x_scales = const.tile([P, UNIT_WORDS], U8, align_bytes=64)
+        nc.vector.quantize_mx(
+            out=x_codes[:].bitcast(FP8X4), scales=x_scales[:], in_=x_grouped[:]
+        )
+
+        def load_first(chunk):
+            tile_ = natural.tile([P, CHUNK_VALUES], BF16, name="nat", tag="nat")
+            by_expert = tile_[:].rearrange("p (e g v) -> p e g v", e=EXPERTS, v=2 * FEATURES)
+            rows = slice(chunk * CHUNK_UNITS * K_PASS, (chunk + 1) * CHUNK_UNITS * K_PASS)
+            for e in range(EXPERTS):
+                nc.sync.dma_start(
+                    out=by_expert[:, e],
+                    in_=first_linear[e, rows, :].rearrange("(g p w) d -> p g (w d)", p=P, w=2),
+                )
+            return tile_[:].bitcast(F32).rearrange(
+                "p (e g w q) -> p e g w q", e=EXPERTS, w=2, q=FEATURES // 2
+            )
+
+        def load_second(chunk):
+            tile_ = natural.tile([P, CHUNK_VALUES], BF16, name="nat", tag="nat")
+            columns = slice(chunk * CHUNK_UNITS * K_PASS, (chunk + 1) * CHUNK_UNITS * K_PASS)
+            nc.sync.dma_start(
+                out=tile_[:].rearrange("p (b i) -> p b i", i=CHUNK_UNITS * K_PASS),
+                in_=second_linear[:, :, columns].rearrange("e (b p) i -> p (e b) i", p=P),
+            )
+            return tile_[:].bitcast(F32).rearrange(
+                "p (e b q) -> p e b q", e=EXPERTS, q=CHUNK_UNITS * K_PASS // 2
+            )
+
+        def first_banks(words, local, j):
+            return [
+                transposed_bank(
+                    lambda u, r, e=e: words[:, e, 2 * local + r, j, u * P : (u + 1) * P],
+                    "raw%d" % e,
+                )
+                for e in range(EXPERTS)
+            ]
+
+        def second_banks(words, local, j):
+            return [
+                transposed_bank(
+                    lambda u, r, e=e: words[
+                        :, e, 2 * j + r, (2 * local + u) * P : (2 * local + u + 1) * P
+                    ],
+                    "raw%d" % e,
+                )
+                for e in range(EXPERTS)
+            ]
+
+        def merge_bank(banks, grouped, j):
+            for pair in range(PAIRS):
+                scaled = work.tile([P, BANK_VALUES], F32, tag="scaled", bufs=4)
+                nc.scalar.activation(
+                    out=by_plane(scaled[:]), in_=banks[1], func=COPY, scale=mixing_weight(pair, 1)
+                )
+                nc.vector.scalar_tensor_tensor(
+                    out=by_plane(grouped[:, pair, j * BANK_VALUES : (j + 1) * BANK_VALUES]),
+                    in0=banks[0],
+                    scalar=mixing_weight(pair, 0),
+                    in1=by_plane(scaled[:]),
+                    op0=MULT,
+                    op1=ADD,
+                )
+
+        def merge_all(load, banks_of, consume):
+            words = load(0)
+            banks = banks_of(words, 0, 0)
+            waiting = None
+            for unit in range(UNITS):
+                grouped = work.tile([P, PAIRS, UNIT_VALUES], BF16, align_bytes=64)
+                for j in range(BANKS_PER_UNIT):
+                    current = banks
+                    if j + 1 < BANKS_PER_UNIT:
+                        banks = banks_of(words, unit % CHUNK_UNITS, j + 1)
+                    elif unit + 1 < UNITS:
+                        if (unit + 1) % CHUNK_UNITS == 0:
+                            words = load((unit + 1) // CHUNK_UNITS)
+                        banks = banks_of(words, (unit + 1) % CHUNK_UNITS, 0)
+                    merge_bank(current, grouped, j)
+                codes = work.tile([P, PAIRS, UNIT_WORDS], U32, align_bytes=64)
+                scales = work.tile([P, PAIRS, UNIT_WORDS], U8, align_bytes=64)
+                for pair in range(PAIRS):
+                    nc.vector.quantize_mx(
+                        out=codes[:, pair, :].bitcast(FP8X4),
+                        scales=scales[:, pair, :],
+                        in_=grouped[:, pair, :],
+                    )
+                if waiting is not None:
+                    consume(*waiting)
+                waiting = (unit, codes, scales)
+            consume(*waiting)
+
+        def h_slot(pair, unit, low, high):
+            first = (pair * UNITS + unit) * P
+            return slice(first + low, first + high)
+
+        with tc.psum_pool(name="hidden_psum", bufs=2) as hidden_psum:
+
+            def hidden_layer(unit, codes, scales):
+                for pair in range(PAIRS):
+                    x_first = token_block(pair) * P
+                    x_columns = slice(x_first, x_first + P)
+                    h_psum = hidden_psum.tile([P, PACK, P], F32)
+                    for t in range(PACK):
+                        block = slice(t * P, (t + 1) * P)
+                        nc.tensor.matmul_mx(
+                            out=h_psum[:, t, :],
+                            lhsT=codes[:, pair, block].bitcast(FP8X4),
+                            lhsT_scale=scales[:, pair, block],
+                            rhs=x_codes[:, x_columns].bitcast(FP8X4),
+                            rhs_scale=x_scales[:, x_columns],
+                            start=True,
+                            stop=True,
+                        )
+                    low, high = token_columns(pair)
+                    h_grouped = work.tile([P, P * PACK], BF16, bufs=4, align_bytes=64)
+                    values = (high - low) * PACK
+                    nc.scalar.activation(
+                        out=h_grouped[:, :values].rearrange("p (k t) -> p k t", t=PACK),
+                        in_=h_psum[:, :, low:high].rearrange("p t k -> p k t"),
+                        func=RELU,
+                    )
+                    slot = h_slot(pair, unit, low, high)
+                    nc.vector.quantize_mx(
+                        out=h_codes[:, slot].bitcast(FP8X4),
+                        scales=h_scales[:, slot],
+                        in_=h_grouped[:, :values],
+                    )
+
+            merge_all(load_first, first_banks, hidden_layer)
+
+        with tc.psum_pool(name="out_psum", bufs=1) as out_psum:
+            sums = [out_psum.tile([P, FEATURES], F32, name="sum%d" % s) for s in range(4)]
+
+            def output_layer(unit, codes, scales):
+                for pair in range(PAIRS):
+                    slot = h_slot(pair, unit, 0, P)
+                    alone = pair < GROUPS
+                    group = pair % GROUPS
+                    nc.tensor.matmul_mx(
+                        out=sums[token_block(pair)][:],
+                        lhsT=h_codes[:, slot].bitcast(FP8X4),
+                        lhsT_scale=h_scales[:, slot],
+                        rhs=codes[:, pair, :].bitcast(FP8X4),
+                        rhs_scale=scales[:, pair, :],
+                        start=unit == 0 and (alone or group == 0),
+                        stop=unit == UNITS - 1 and (alone or group == GROUPS - 1),
+                    )
+
+            merge_all(load_second, second_banks, output_layer)
+
+            for s in range(4):
+                result = work.tile([P, FEATURES], F32)
+                nc.scalar.copy(out=result[:], in_=sums[s][:])
+                if s < GROUPS:
+                    for segment in range(2):
+                        first = segment * P + s * GROUP_ROWS
+                        nc.sync.dma_start(
+                            out=out_rows[first : first + GROUP_ROWS, :],
+                            in_=result[segment * GROUP_ROWS : (segment + 1) * GROUP_ROWS, :],
+                        )
+                else:
+                    nc.sync.dma_start(out=out_rows[s * P : (s + 1) * P, :], in_=result[:])

@@ -29,8 +29,7 @@ BANK_VALUES = 2 * BANK_WORDS
 BANKS_PER_UNIT = 2
 UNIT_VALUES = BANKS_PER_UNIT * BANK_VALUES
 UNIT_WORDS = UNIT_VALUES // PACK
-CHUNK_UNITS = 2
-CHUNK_VALUES = EXPERTS * CHUNK_UNITS * UNIT_VALUES
+ROUND = 5
 
 FLOPS = 2 * 2 * 512 * FEATURES * HIDDEN
 
@@ -44,6 +43,7 @@ def tile_mh_lori_pa_k_kernel(tc, x_mh, ew, first_linear, second_linear, out):
         const = ctx.enter_context(tc.tile_pool(name="const", bufs=1))
         natural = ctx.enter_context(tc.tile_pool(name="natural", bufs=2))
         work = ctx.enter_context(tc.tile_pool(name="work", bufs=2))
+        slow = ctx.enter_context(tc.tile_pool(name="slow", bufs=1))
         raw_psum = ctx.enter_context(tc.psum_pool(name="raw_psum", bufs=2))
 
         identity = const.tile([P, P], F32)
@@ -102,120 +102,153 @@ def tile_mh_lori_pa_k_kernel(tc, x_mh, ew, first_linear, second_linear, out):
         def by_plane(flat):
             return flat.rearrange("p (c u) -> p c u", u=2)
 
-        x_natural = const.tile([P, 4 * FEATURES], BF16)
-        x_blocks = x_natural[:].rearrange("p (k d) -> p k d", d=FEATURES)
-        for segment in range(2):
-            nc.sync.dma_start(
-                out=x_blocks[segment * GROUP_ROWS : (segment + 1) * GROUP_ROWS, 0:2, :],
-                in_=x_rows[segment * P : (segment + 1) * P, :].rearrange(
-                    "(g j) d -> j g d", g=GROUPS
-                ),
-            )
-        nc.sync.dma_start(
-            out=x_blocks[:, 2:4, :],
-            in_=x_rows[2 * P : 4 * P, :].rearrange("(k p) d -> p k d", p=P),
-        )
-        x_words = x_natural[:].bitcast(F32).rearrange("p (k q) -> p k q", q=FEATURES // 2)
-        x_grouped = const.tile([P, UNIT_VALUES], BF16, align_bytes=64)
-        for j in range(BANKS_PER_UNIT):
-            bank = transposed_bank(
-                lambda u, r, j=j: x_words[:, 2 * j + r, u * P : (u + 1) * P], "raw0"
-            )
-            nc.vector.tensor_copy(
-                out=by_plane(x_grouped[:, j * BANK_VALUES : (j + 1) * BANK_VALUES]), in_=bank
-            )
+        def bank_values(j):
+            return slice(j * BANK_VALUES, (j + 1) * BANK_VALUES)
+
         x_codes = const.tile([P, UNIT_WORDS], U32, align_bytes=64)
         x_scales = const.tile([P, UNIT_WORDS], U8, align_bytes=64)
-        nc.vector.quantize_mx(
-            out=x_codes[:].bitcast(FP8X4), scales=x_scales[:], in_=x_grouped[:]
-        )
+        with tc.tile_pool(name="x_stage", bufs=1) as x_stage:
+            x_natural = x_stage.tile([P, 4 * FEATURES], BF16)
+            x_blocks = x_natural[:].rearrange("p (k d) -> p k d", d=FEATURES)
+            for segment in range(2):
+                nc.sync.dma_start(
+                    out=x_blocks[segment * GROUP_ROWS : (segment + 1) * GROUP_ROWS, 0:2, :],
+                    in_=x_rows[segment * P : (segment + 1) * P, :].rearrange(
+                        "(g j) d -> j g d", g=GROUPS
+                    ),
+                )
+            nc.sync.dma_start(
+                out=x_blocks[:, 2:4, :],
+                in_=x_rows[2 * P : 4 * P, :].rearrange("(k p) d -> p k d", p=P),
+            )
+            x_words = x_natural[:].bitcast(F32).rearrange("p (k q) -> p k q", q=FEATURES // 2)
+            x_grouped = x_stage.tile([P, UNIT_VALUES], BF16, align_bytes=64)
+            for j in range(BANKS_PER_UNIT):
+                bank = transposed_bank(
+                    lambda u, r, j=j: x_words[:, 2 * j + r, u * P : (u + 1) * P], "raw0"
+                )
+                nc.vector.tensor_copy(out=by_plane(x_grouped[:, bank_values(j)]), in_=bank)
+            nc.vector.quantize_mx(
+                out=x_codes[:].bitcast(FP8X4), scales=x_scales[:], in_=x_grouped[:]
+            )
 
-        def load_first(chunk):
-            tile_ = natural.tile([P, CHUNK_VALUES], BF16, name="nat", tag="nat")
-            by_expert = tile_[:].rearrange("p (e g v) -> p e g v", e=EXPERTS, v=2 * FEATURES)
-            rows = slice(chunk * CHUNK_UNITS * K_PASS, (chunk + 1) * CHUNK_UNITS * K_PASS)
+        def first_blocks(unit):
+            loaded = natural.tile([P, EXPERTS * UNIT_VALUES], BF16, name="nat", tag="nat")
+            by_expert = loaded[:].rearrange("p (e r v) -> p e r v", e=EXPERTS, v=2 * FEATURES)
+            rows = slice(unit * K_PASS, (unit + 1) * K_PASS)
             for e in range(EXPERTS):
                 nc.sync.dma_start(
                     out=by_expert[:, e],
-                    in_=first_linear[e, rows, :].rearrange("(g p w) d -> p g (w d)", p=P, w=2),
+                    in_=first_linear[e, rows, :].rearrange("(r p j) d -> p r (j d)", p=P, j=2),
                 )
-            return tile_[:].bitcast(F32).rearrange(
-                "p (e g w q) -> p e g w q", e=EXPERTS, w=2, q=FEATURES // 2
+            words = loaded[:].bitcast(F32).rearrange(
+                "p (e r j q) -> p e r j q", e=EXPERTS, j=2, q=FEATURES // 2
             )
+            return lambda e, j, u, r: words[:, e, r, j, u * P : (u + 1) * P]
 
-        def load_second(chunk):
-            tile_ = natural.tile([P, CHUNK_VALUES], BF16, name="nat", tag="nat")
-            columns = slice(chunk * CHUNK_UNITS * K_PASS, (chunk + 1) * CHUNK_UNITS * K_PASS)
+        def second_blocks(unit):
+            loaded = natural.tile([P, EXPERTS * UNIT_VALUES], BF16, name="nat", tag="nat")
+            columns = slice(unit * K_PASS, (unit + 1) * K_PASS)
             nc.sync.dma_start(
-                out=tile_[:].rearrange("p (b i) -> p b i", i=CHUNK_UNITS * K_PASS),
+                out=loaded[:].rearrange("p (b i) -> p b i", i=K_PASS),
                 in_=second_linear[:, :, columns].rearrange("e (b p) i -> p (e b) i", p=P),
             )
-            return tile_[:].bitcast(F32).rearrange(
-                "p (e b q) -> p e b q", e=EXPERTS, q=CHUNK_UNITS * K_PASS // 2
+            words = loaded[:].bitcast(F32).rearrange(
+                "p (e b q) -> p e b q", e=EXPERTS, q=K_PASS // 2
             )
+            return lambda e, j, u, r: words[:, e, 2 * j + r, u * P : (u + 1) * P]
 
-        def first_banks(words, local, j):
+        def transposed_experts(blocks, j):
             return [
-                transposed_bank(
-                    lambda u, r, e=e: words[:, e, 2 * local + r, j, u * P : (u + 1) * P],
-                    "raw%d" % e,
-                )
+                transposed_bank(lambda u, r, e=e: blocks(e, j, u, r), "raw%d" % e)
                 for e in range(EXPERTS)
             ]
 
-        def second_banks(words, local, j):
-            return [
-                transposed_bank(
-                    lambda u, r, e=e: words[
-                        :, e, 2 * j + r, (2 * local + u) * P : (2 * local + u + 1) * P
-                    ],
-                    "raw%d" % e,
-                )
-                for e in range(EXPERTS)
-            ]
+        def new_operand():
+            codes = work.tile([P, PAIRS, UNIT_WORDS], U32, align_bytes=64)
+            scales = work.tile([P, PAIRS, UNIT_WORDS], U8, align_bytes=64)
+            return codes, scales
 
-        def merge_bank(banks, grouped, j):
-            for pair in range(PAIRS):
-                scaled = work.tile([P, BANK_VALUES], F32, tag="scaled", bufs=4)
-                nc.scalar.activation(
-                    out=by_plane(scaled[:]), in_=banks[1], func=COPY, scale=mixing_weight(pair, 1)
-                )
-                nc.vector.scalar_tensor_tensor(
-                    out=by_plane(grouped[:, pair, j * BANK_VALUES : (j + 1) * BANK_VALUES]),
-                    in0=banks[0],
-                    scalar=mixing_weight(pair, 0),
-                    in1=by_plane(scaled[:]),
-                    op0=MULT,
-                    op1=ADD,
-                )
-
-        def merge_all(load, banks_of, consume):
-            words = load(0)
-            banks = banks_of(words, 0, 0)
-            waiting = None
-            for unit in range(UNITS):
-                grouped = work.tile([P, PAIRS, UNIT_VALUES], BF16, align_bytes=64)
-                for j in range(BANKS_PER_UNIT):
-                    current = banks
-                    if j + 1 < BANKS_PER_UNIT:
-                        banks = banks_of(words, unit % CHUNK_UNITS, j + 1)
-                    elif unit + 1 < UNITS:
-                        if (unit + 1) % CHUNK_UNITS == 0:
-                            words = load((unit + 1) // CHUNK_UNITS)
-                        banks = banks_of(words, (unit + 1) % CHUNK_UNITS, 0)
-                    merge_bank(current, grouped, j)
-                codes = work.tile([P, PAIRS, UNIT_WORDS], U32, align_bytes=64)
-                scales = work.tile([P, PAIRS, UNIT_WORDS], U8, align_bytes=64)
+        def merge_on_vector(blocks):
+            codes, scales = new_operand()
+            for j in range(BANKS_PER_UNIT):
+                raw = transposed_experts(blocks, j)
+                grouped = work.tile([P, PAIRS, BANK_VALUES], BF16, align_bytes=64)
+                for pair in range(PAIRS):
+                    scaled = work.tile([P, BANK_VALUES], F32, bufs=4)
+                    nc.scalar.activation(
+                        out=by_plane(scaled[:]),
+                        in_=raw[1],
+                        func=COPY,
+                        scale=mixing_weight(pair, 1),
+                    )
+                    nc.vector.scalar_tensor_tensor(
+                        out=by_plane(grouped[:, pair, :]),
+                        in0=raw[0],
+                        scalar=mixing_weight(pair, 0),
+                        in1=by_plane(scaled[:]),
+                        op0=MULT,
+                        op1=ADD,
+                    )
+                words = slice(j * BANK_VALUES // PACK, (j + 1) * BANK_VALUES // PACK)
                 for pair in range(PAIRS):
                     nc.vector.quantize_mx(
-                        out=codes[:, pair, :].bitcast(FP8X4),
-                        scales=scales[:, pair, :],
+                        out=codes[:, pair, words].bitcast(FP8X4),
+                        scales=scales[:, pair, words],
                         in_=grouped[:, pair, :],
                     )
-                if waiting is not None:
-                    consume(*waiting)
-                waiting = (unit, codes, scales)
-            consume(*waiting)
+            return codes, scales
+
+        def copy_for_gpsimd(blocks):
+            copies = slow.tile([P, EXPERTS, UNIT_VALUES], BF16, bufs=2)
+            for j in range(BANKS_PER_UNIT):
+                raw = transposed_experts(blocks, j)
+                for e in range(EXPERTS):
+                    nc.scalar.copy(out=by_plane(copies[:, e, bank_values(j)]), in_=raw[e])
+            return copies
+
+        def merge_on_gpsimd(copies):
+            merged = slow.tile([P, PAIRS, UNIT_VALUES], BF16, align_bytes=64)
+            for pair in range(PAIRS):
+                parts = []
+                for e in range(EXPERTS):
+                    part = slow.tile([P, UNIT_VALUES], F32, name="part%d" % e, tag="part%d" % e)
+                    nc.gpsimd.tensor_scalar(
+                        out=part[:],
+                        in0=copies[:, e, :],
+                        scalar1=mixing_weight(pair, e),
+                        scalar2=0.0,
+                        op0=MULT,
+                        op1=ADD,
+                    )
+                    parts.append(part)
+                nc.gpsimd.tensor_tensor(
+                    out=merged[:, pair, :], in0=parts[0][:], in1=parts[1][:], op=ADD
+                )
+            return merged
+
+        def quantise_unit(merged):
+            codes, scales = new_operand()
+            for pair in range(PAIRS):
+                nc.vector.quantize_mx(
+                    out=codes[:, pair, :].bitcast(FP8X4),
+                    scales=scales[:, pair, :],
+                    in_=merged[:, pair, :],
+                )
+            return codes, scales
+
+        def all_units(blocks_of, consume):
+            copies = copy_for_gpsimd(blocks_of(ROUND - 1))
+            for first in range(0, UNITS, ROUND):
+                last = first + ROUND - 1
+                if last < UNITS:
+                    merged = merge_on_gpsimd(copies)
+                    if last + ROUND < UNITS:
+                        copies = copy_for_gpsimd(blocks_of(last + ROUND))
+                for unit in range(first, min(last, UNITS)):
+                    consume(unit, *merge_on_vector(blocks_of(unit)))
+                if last < UNITS:
+                    consume(last, *quantise_unit(merged))
 
         def h_slot(pair, unit, low, high):
             first = (pair * UNITS + unit) * P
@@ -254,7 +287,7 @@ def tile_mh_lori_pa_k_kernel(tc, x_mh, ew, first_linear, second_linear, out):
                         in_=h_grouped[:, :values],
                     )
 
-            merge_all(load_first, first_banks, hidden_layer)
+            all_units(first_blocks, hidden_layer)
 
         with tc.psum_pool(name="out_psum", bufs=1) as out_psum:
             sums = [out_psum.tile([P, FEATURES], F32, name="sum%d" % s) for s in range(4)]
@@ -274,7 +307,7 @@ def tile_mh_lori_pa_k_kernel(tc, x_mh, ew, first_linear, second_linear, out):
                         stop=unit == UNITS - 1 and (alone or group == GROUPS - 1),
                     )
 
-            merge_all(load_second, second_banks, output_layer)
+            all_units(second_blocks, output_layer)
 
             for s in range(4):
                 result = work.tile([P, FEATURES], F32)

@@ -20,18 +20,38 @@ K_PASS = P * PACK
 EXPERTS = 2
 GROUPS = 2
 GROUP_ROWS = 64
+HEAD_VECTORS = 512
+TOKEN_BLOCKS = HEAD_VECTORS // P
 FEATURES = 512
 HIDDEN = 8192
 UNITS = HIDDEN // K_PASS
 PAIRS = 6
 BANK_WORDS = 512
 BANK_VALUES = 2 * BANK_WORDS
-BANKS_PER_UNIT = 2
-UNIT_VALUES = BANKS_PER_UNIT * BANK_VALUES
+BANK_COLUMNS = BANK_VALUES // PACK
+UNIT_VALUES = K_PASS * K_PASS // P
+UNIT_BANKS = UNIT_VALUES // BANK_VALUES
 UNIT_WORDS = UNIT_VALUES // PACK
-ROUND = 5
 
-FLOPS = 2 * 2 * 512 * FEATURES * HIDDEN
+FLOPS = 2 * 2 * HEAD_VECTORS * FEATURES * HIDDEN
+
+
+def token_block(pair):
+    weight_segment, group = divmod(pair, GROUPS)
+    return group if weight_segment == 0 else weight_segment + 1
+
+
+def token_columns(pair):
+    weight_segment, group = divmod(pair, GROUPS)
+    if weight_segment == 0:
+        return 0, P
+    return group * GROUP_ROWS, (group + 1) * GROUP_ROWS
+
+
+def block_rows(block):
+    if block < GROUPS:
+        return [(s * GROUP_ROWS, s * P + block * GROUP_ROWS, GROUP_ROWS) for s in range(2)]
+    return [(0, block * P, P)]
 
 
 def tile_mh_lori_pa_k_kernel(tc, x_mh, ew, first_linear, second_linear, out):
@@ -41,9 +61,8 @@ def tile_mh_lori_pa_k_kernel(tc, x_mh, ew, first_linear, second_linear, out):
 
     with ExitStack() as ctx:
         const = ctx.enter_context(tc.tile_pool(name="const", bufs=1))
-        natural = ctx.enter_context(tc.tile_pool(name="natural", bufs=2))
+        natural = ctx.enter_context(tc.tile_pool(name="natural", bufs=3))
         work = ctx.enter_context(tc.tile_pool(name="work", bufs=2))
-        slow = ctx.enter_context(tc.tile_pool(name="slow", bufs=1))
         raw_psum = ctx.enter_context(tc.psum_pool(name="raw_psum", bufs=2))
 
         identity = const.tile([P, P], F32)
@@ -60,221 +79,141 @@ def tile_mh_lori_pa_k_kernel(tc, x_mh, ew, first_linear, second_linear, out):
             column = EXPERTS * pair + expert
             return ew_f32[:, column : column + 1]
 
-        h_codes = const.tile([P, PAIRS * UNITS * P], U32, align_bytes=64)
-        h_scales = const.tile([P, PAIRS * UNITS * P], U8, align_bytes=64)
-
-        def token_columns(pair):
-            if pair < GROUPS:
-                return 0, P
-            group = pair % GROUPS
-            return group * GROUP_ROWS, (group + 1) * GROUP_ROWS
-
-        def token_block(pair):
-            weight_segment, group = divmod(pair, GROUPS)
-            return group if weight_segment == 0 else weight_segment + 1
-
-        for pair in range(GROUPS, PAIRS):
-            zero_low = GROUP_ROWS - token_columns(pair)[0]
-            pair_words = slice(pair * UNITS * P, (pair + 1) * UNITS * P)
-            nc.vector.memset(
-                h_codes[:, pair_words]
-                .bitcast(I32)
-                .rearrange("p (n k) -> p n k", k=P)[:, :, zero_low : zero_low + GROUP_ROWS],
-                0,
-            )
-            nc.vector.memset(
-                h_scales[:, pair_words]
-                .bitcast(I32)
-                .rearrange("p (n k) -> p n k", k=P // 4)[
-                    :, :, zero_low // 4 : (zero_low + GROUP_ROWS) // 4
-                ],
-                0,
-            )
-
-        def transposed_bank(block_of, tag):
+        def transposed_bank(words, tag):
             bank = raw_psum.tile([P, BANK_WORDS], F32, name=tag, tag=tag)
+            blocks = bank[:].rearrange("p (u r c) -> p u r c", u=2, r=2)
             for u in range(2):
                 for r in range(2):
-                    first = (2 * u + r) * P
-                    nc.tensor.transpose(bank[:, first : first + P], block_of(u, r), identity[:])
+                    nc.tensor.transpose(blocks[:, u, r, :], words[:, u, r, :], identity[:])
             return bank[:].bitcast(BF16).rearrange("p (u c) -> p c u", u=2)
 
-        def by_plane(flat):
+        def like_bank(flat):
             return flat.rearrange("p (c u) -> p c u", u=2)
 
         def bank_values(j):
             return slice(j * BANK_VALUES, (j + 1) * BANK_VALUES)
 
-        x_codes = const.tile([P, UNIT_WORDS], U32, align_bytes=64)
-        x_scales = const.tile([P, UNIT_WORDS], U8, align_bytes=64)
+        x_codes = const.tile([P, HEAD_VECTORS], U32, align_bytes=64)
+        x_scales = const.tile([P, HEAD_VECTORS], U8, align_bytes=64)
         with tc.tile_pool(name="x_stage", bufs=1) as x_stage:
-            x_natural = x_stage.tile([P, 4 * FEATURES], BF16)
+            x_natural = x_stage.tile([P, TOKEN_BLOCKS * FEATURES], BF16)
             x_blocks = x_natural[:].rearrange("p (k d) -> p k d", d=FEATURES)
-            for segment in range(2):
-                nc.sync.dma_start(
-                    out=x_blocks[segment * GROUP_ROWS : (segment + 1) * GROUP_ROWS, 0:2, :],
-                    in_=x_rows[segment * P : (segment + 1) * P, :].rearrange(
-                        "(g j) d -> j g d", g=GROUPS
-                    ),
-                )
-            nc.sync.dma_start(
-                out=x_blocks[:, 2:4, :],
-                in_=x_rows[2 * P : 4 * P, :].rearrange("(k p) d -> p k d", p=P),
+            for block in range(TOKEN_BLOCKS):
+                for partition, row, count in block_rows(block):
+                    nc.sync.dma_start(
+                        out=x_blocks[partition : partition + count, block, :],
+                        in_=x_rows[row : row + count, :],
+                    )
+            x_words = x_natural[:].bitcast(F32).rearrange(
+                "p (j r u q) -> p j u r q", r=2, u=2, q=P
             )
-            x_words = x_natural[:].bitcast(F32).rearrange("p (k q) -> p k q", q=FEATURES // 2)
-            x_grouped = x_stage.tile([P, UNIT_VALUES], BF16, align_bytes=64)
-            for j in range(BANKS_PER_UNIT):
-                bank = transposed_bank(
-                    lambda u, r, j=j: x_words[:, 2 * j + r, u * P : (u + 1) * P], "raw0"
-                )
-                nc.vector.tensor_copy(out=by_plane(x_grouped[:, bank_values(j)]), in_=bank)
+            x_grouped = x_stage.tile([P, PACK * HEAD_VECTORS], BF16, align_bytes=64)
+            for j in range(HEAD_VECTORS // BANK_COLUMNS):
+                bank = transposed_bank(x_words[:, j], "raw0")
+                nc.vector.tensor_copy(out=like_bank(x_grouped[:, bank_values(j)]), in_=bank)
             nc.vector.quantize_mx(
                 out=x_codes[:].bitcast(FP8X4), scales=x_scales[:], in_=x_grouped[:]
             )
 
-        def first_blocks(unit):
-            loaded = natural.tile([P, EXPERTS * UNIT_VALUES], BF16, name="nat", tag="nat")
-            by_expert = loaded[:].rearrange("p (e r v) -> p e r v", e=EXPERTS, v=2 * FEATURES)
+        h_codes = const.tile([P, PAIRS * UNITS * P], U32, align_bytes=64)
+        h_scales = const.tile([P, PAIRS * UNITS * P], U8, align_bytes=64)
+
+        def h_slot(pair, unit, low, high):
+            first = (pair * UNITS + unit) * P
+            return slice(first + low, first + high)
+
+        for pair in range(GROUPS, PAIRS):
+            other_low = GROUP_ROWS - token_columns(pair)[0]
+            all_units = h_slot(pair, 0, 0, UNITS * P)
+            nc.vector.memset(
+                h_codes[:, all_units]
+                .bitcast(I32)
+                .rearrange("p (n k) -> p n k", k=P)[:, :, other_low : other_low + GROUP_ROWS],
+                0,
+            )
+            nc.vector.memset(
+                h_scales[:, all_units]
+                .bitcast(I32)
+                .rearrange("p (n k) -> p n k", k=P // 4)[
+                    :, :, other_low // 4 : (other_low + GROUP_ROWS) // 4
+                ],
+                0,
+            )
+
+        def load_first(unit):
+            loaded = natural.tile([P, EXPERTS * UNIT_VALUES], BF16, name="loaded", tag="loaded")
+            by_expert = loaded[:].rearrange("p (e r v) -> p e r v", e=EXPERTS, r=2)
             rows = slice(unit * K_PASS, (unit + 1) * K_PASS)
             for e in range(EXPERTS):
                 nc.sync.dma_start(
                     out=by_expert[:, e],
                     in_=first_linear[e, rows, :].rearrange("(r p j) d -> p r (j d)", p=P, j=2),
                 )
-            words = loaded[:].bitcast(F32).rearrange(
-                "p (e r j q) -> p e r j q", e=EXPERTS, j=2, q=FEATURES // 2
+            return loaded[:].bitcast(F32).rearrange(
+                "p (e r j u q) -> p e j u r q", e=EXPERTS, r=2, j=2, u=2
             )
-            return lambda e, j, u, r: words[:, e, r, j, u * P : (u + 1) * P]
 
-        def second_blocks(unit):
-            loaded = natural.tile([P, EXPERTS * UNIT_VALUES], BF16, name="nat", tag="nat")
+        def load_second(unit):
+            loaded = natural.tile([P, EXPERTS * UNIT_VALUES], BF16, name="loaded", tag="loaded")
             columns = slice(unit * K_PASS, (unit + 1) * K_PASS)
             nc.sync.dma_start(
                 out=loaded[:].rearrange("p (b i) -> p b i", i=K_PASS),
                 in_=second_linear[:, :, columns].rearrange("e (b p) i -> p (e b) i", p=P),
             )
-            words = loaded[:].bitcast(F32).rearrange(
-                "p (e b q) -> p e b q", e=EXPERTS, q=K_PASS // 2
+            return loaded[:].bitcast(F32).rearrange(
+                "p (e j r u q) -> p e j u r q", e=EXPERTS, j=2, r=2, u=2
             )
-            return lambda e, j, u, r: words[:, e, 2 * j + r, u * P : (u + 1) * P]
 
-        def transposed_experts(blocks, j):
-            return [
-                transposed_bank(lambda u, r, e=e: blocks(e, j, u, r), "raw%d" % e)
-                for e in range(EXPERTS)
-            ]
-
-        def new_operand():
-            codes = work.tile([P, PAIRS, UNIT_WORDS], U32, align_bytes=64)
-            scales = work.tile([P, PAIRS, UNIT_WORDS], U8, align_bytes=64)
-            return codes, scales
-
-        def merge_on_vector(blocks):
-            codes, scales = new_operand()
-            for j in range(BANKS_PER_UNIT):
-                raw = transposed_experts(blocks, j)
-                grouped = work.tile([P, PAIRS, BANK_VALUES], BF16, align_bytes=64)
+        def merged_unit(words):
+            grouped = work.tile([P, PAIRS, UNIT_VALUES], BF16, align_bytes=64)
+            for j in range(UNIT_BANKS):
+                raw = [transposed_bank(words[:, e, j], "raw%d" % e) for e in range(EXPERTS)]
                 for pair in range(PAIRS):
                     scaled = work.tile([P, BANK_VALUES], F32, bufs=4)
                     nc.scalar.activation(
-                        out=by_plane(scaled[:]),
+                        out=like_bank(scaled[:]),
                         in_=raw[1],
                         func=COPY,
                         scale=mixing_weight(pair, 1),
                     )
                     nc.vector.scalar_tensor_tensor(
-                        out=by_plane(grouped[:, pair, :]),
+                        out=like_bank(grouped[:, pair, bank_values(j)]),
                         in0=raw[0],
                         scalar=mixing_weight(pair, 0),
-                        in1=by_plane(scaled[:]),
+                        in1=like_bank(scaled[:]),
                         op0=MULT,
                         op1=ADD,
                     )
-                words = slice(j * BANK_VALUES // PACK, (j + 1) * BANK_VALUES // PACK)
-                for pair in range(PAIRS):
-                    nc.vector.quantize_mx(
-                        out=codes[:, pair, words].bitcast(FP8X4),
-                        scales=scales[:, pair, words],
-                        in_=grouped[:, pair, :],
-                    )
-            return codes, scales
-
-        def copy_for_gpsimd(blocks):
-            copies = slow.tile([P, EXPERTS, UNIT_VALUES], BF16, bufs=2)
-            for j in range(BANKS_PER_UNIT):
-                raw = transposed_experts(blocks, j)
-                for e in range(EXPERTS):
-                    nc.scalar.copy(out=by_plane(copies[:, e, bank_values(j)]), in_=raw[e])
-            return copies
-
-        def merge_on_gpsimd(copies):
-            merged = slow.tile([P, PAIRS, UNIT_VALUES], BF16, align_bytes=64)
-            for pair in range(PAIRS):
-                parts = []
-                for e in range(EXPERTS):
-                    part = slow.tile([P, UNIT_VALUES], F32, name="part%d" % e, tag="part%d" % e)
-                    nc.gpsimd.tensor_scalar(
-                        out=part[:],
-                        in0=copies[:, e, :],
-                        scalar1=mixing_weight(pair, e),
-                        scalar2=0.0,
-                        op0=MULT,
-                        op1=ADD,
-                    )
-                    parts.append(part)
-                nc.gpsimd.tensor_tensor(
-                    out=merged[:, pair, :], in0=parts[0][:], in1=parts[1][:], op=ADD
-                )
-            return merged
-
-        def quantise_unit(merged):
-            codes, scales = new_operand()
+            codes = work.tile([P, PAIRS, UNIT_WORDS], U32, align_bytes=64)
+            scales = work.tile([P, PAIRS, UNIT_WORDS], U8, align_bytes=64)
             for pair in range(PAIRS):
                 nc.vector.quantize_mx(
                     out=codes[:, pair, :].bitcast(FP8X4),
                     scales=scales[:, pair, :],
-                    in_=merged[:, pair, :],
+                    in_=grouped[:, pair, :],
                 )
             return codes, scales
 
-        def all_units(blocks_of, consume):
-            copies = copy_for_gpsimd(blocks_of(ROUND - 1))
-            for first in range(0, UNITS, ROUND):
-                last = first + ROUND - 1
-                if last < UNITS:
-                    merged = merge_on_gpsimd(copies)
-                    if last + ROUND < UNITS:
-                        copies = copy_for_gpsimd(blocks_of(last + ROUND))
-                for unit in range(first, min(last, UNITS)):
-                    consume(unit, *merge_on_vector(blocks_of(unit)))
-                if last < UNITS:
-                    consume(last, *quantise_unit(merged))
-
-        def h_slot(pair, unit, low, high):
-            first = (pair * UNITS + unit) * P
-            return slice(first + low, first + high)
-
         with tc.psum_pool(name="hidden_psum", bufs=2) as hidden_psum:
-
-            def hidden_layer(unit, codes, scales):
+            for unit in range(UNITS):
+                codes, scales = merged_unit(load_first(unit))
                 for pair in range(PAIRS):
-                    x_first = token_block(pair) * P
-                    x_columns = slice(x_first, x_first + P)
+                    tokens = slice(token_block(pair) * P, (token_block(pair) + 1) * P)
                     h_psum = hidden_psum.tile([P, PACK, P], F32)
                     for t in range(PACK):
-                        block = slice(t * P, (t + 1) * P)
+                        hidden_units = slice(t * P, (t + 1) * P)
                         nc.tensor.matmul_mx(
                             out=h_psum[:, t, :],
-                            lhsT=codes[:, pair, block].bitcast(FP8X4),
-                            lhsT_scale=scales[:, pair, block],
-                            rhs=x_codes[:, x_columns].bitcast(FP8X4),
-                            rhs_scale=x_scales[:, x_columns],
+                            lhsT=codes[:, pair, hidden_units].bitcast(FP8X4),
+                            lhsT_scale=scales[:, pair, hidden_units],
+                            rhs=x_codes[:, tokens].bitcast(FP8X4),
+                            rhs_scale=x_scales[:, tokens],
                             start=True,
                             stop=True,
                         )
                     low, high = token_columns(pair)
-                    h_grouped = work.tile([P, P * PACK], BF16, bufs=4, align_bytes=64)
                     values = (high - low) * PACK
+                    h_grouped = work.tile([P, P * PACK], BF16, bufs=4, align_bytes=64)
                     nc.scalar.activation(
                         out=h_grouped[:, :values].rearrange("p (k t) -> p k t", t=PACK),
                         in_=h_psum[:, :, low:high].rearrange("p t k -> p k t"),
@@ -287,37 +226,31 @@ def tile_mh_lori_pa_k_kernel(tc, x_mh, ew, first_linear, second_linear, out):
                         in_=h_grouped[:, :values],
                     )
 
-            all_units(first_blocks, hidden_layer)
-
         with tc.psum_pool(name="out_psum", bufs=1) as out_psum:
-            sums = [out_psum.tile([P, FEATURES], F32, name="sum%d" % s) for s in range(4)]
-
-            def output_layer(unit, codes, scales):
+            sums = [
+                out_psum.tile([P, FEATURES], F32, name="sum%d" % block)
+                for block in range(TOKEN_BLOCKS)
+            ]
+            for unit in range(UNITS):
+                codes, scales = merged_unit(load_second(unit))
                 for pair in range(PAIRS):
+                    low, high = token_columns(pair)
                     slot = h_slot(pair, unit, 0, P)
-                    alone = pair < GROUPS
-                    group = pair % GROUPS
                     nc.tensor.matmul_mx(
                         out=sums[token_block(pair)][:],
                         lhsT=h_codes[:, slot].bitcast(FP8X4),
                         lhsT_scale=h_scales[:, slot],
                         rhs=codes[:, pair, :].bitcast(FP8X4),
                         rhs_scale=scales[:, pair, :],
-                        start=unit == 0 and (alone or group == 0),
-                        stop=unit == UNITS - 1 and (alone or group == GROUPS - 1),
+                        start=unit == 0 and low == 0,
+                        stop=unit == UNITS - 1 and high == P,
                     )
 
-            all_units(second_blocks, output_layer)
-
-            for s in range(4):
+            for block in range(TOKEN_BLOCKS):
                 result = work.tile([P, FEATURES], F32)
-                nc.scalar.copy(out=result[:], in_=sums[s][:])
-                if s < GROUPS:
-                    for segment in range(2):
-                        first = segment * P + s * GROUP_ROWS
-                        nc.sync.dma_start(
-                            out=out_rows[first : first + GROUP_ROWS, :],
-                            in_=result[segment * GROUP_ROWS : (segment + 1) * GROUP_ROWS, :],
-                        )
-                else:
-                    nc.sync.dma_start(out=out_rows[s * P : (s + 1) * P, :], in_=result[:])
+                nc.scalar.copy(out=result[:], in_=sums[block][:])
+                for partition, row, count in block_rows(block):
+                    nc.sync.dma_start(
+                        out=out_rows[row : row + count, :],
+                        in_=result[partition : partition + count, :],
+                    )

from contextlib import ExitStack

import concourse.mybir as mybir
from concourse.masks import make_identity

BF16 = mybir.dt.bfloat16
F32 = mybir.dt.float32
I32 = mybir.dt.int32
U32 = mybir.dt.uint32
U8 = mybir.dt.uint8
FP8X4 = mybir.dt.float8_e4m3fn_x4
MULT = mybir.AluOpType.mult
ADD = mybir.AluOpType.add
COPY = mybir.ActivationFunctionType.Copy
RELU = mybir.ActivationFunctionType.Relu

P = 128
PACK = 4
K_PASS = P * PACK
EXPERTS = 2
GROUPS = 2
GROUP_ROWS = 64
HEAD_VECTORS = 512
TOKEN_BLOCKS = HEAD_VECTORS // P
FEATURES = 512
HIDDEN = 8192
UNITS = HIDDEN // K_PASS
PAIRS = 6
BANK_WORDS = 512
BANK_VALUES = 2 * BANK_WORDS
BANK_COLUMNS = BANK_VALUES // PACK
UNIT_VALUES = K_PASS * K_PASS // P
UNIT_BANKS = UNIT_VALUES // BANK_VALUES
UNIT_WORDS = UNIT_VALUES // PACK

FLOPS = 2 * 2 * HEAD_VECTORS * FEATURES * HIDDEN


def token_block(pair):
    weight_segment, group = divmod(pair, GROUPS)
    return group if weight_segment == 0 else weight_segment + 1


def token_columns(pair):
    weight_segment, group = divmod(pair, GROUPS)
    if weight_segment == 0:
        return 0, P
    return group * GROUP_ROWS, (group + 1) * GROUP_ROWS


def block_rows(block):
    if block < GROUPS:
        return [(s * GROUP_ROWS, s * P + block * GROUP_ROWS, GROUP_ROWS) for s in range(2)]
    return [(0, block * P, P)]


def tile_mh_lori_pa_k_kernel(tc, x_mh, ew, first_linear, second_linear, out):
    nc = tc.nc
    x_rows = x_mh.rearrange("b s (h d) -> (b s h) d", d=FEATURES)
    out_rows = out.rearrange("b s (h d) -> (b s h) d", d=FEATURES)

    with ExitStack() as ctx:
        const = ctx.enter_context(tc.tile_pool(name="const", bufs=1))
        natural = ctx.enter_context(tc.tile_pool(name="natural", bufs=3))
        work = ctx.enter_context(tc.tile_pool(name="work", bufs=2))
        raw_psum = ctx.enter_context(tc.psum_pool(name="raw_psum", bufs=2))

        identity = const.tile([P, P], F32)
        make_identity(nc, identity[:])

        ew_bf16 = const.tile([P, PAIRS * EXPERTS], BF16)
        nc.sync.dma_start(
            out=ew_bf16[:], in_=ew.rearrange("b n g e -> (b n g e)").partition_broadcast(P)
        )
        ew_f32 = const.tile([P, PAIRS * EXPERTS], F32)
        nc.vector.tensor_copy(out=ew_f32[:], in_=ew_bf16[:])

        def mixing_weight(pair, expert):
            column = EXPERTS * pair + expert
            return ew_f32[:, column : column + 1]

        def transposed_bank(words, tag):
            bank = raw_psum.tile([P, BANK_WORDS], F32, name=tag, tag=tag)
            blocks = bank[:].rearrange("p (u r c) -> p u r c", u=2, r=2)
            for u in range(2):
                for r in range(2):
                    nc.tensor.transpose(blocks[:, u, r, :], words[:, u, r, :], identity[:])
            return bank[:].bitcast(BF16).rearrange("p (u c) -> p c u", u=2)

        def like_bank(flat):
            return flat.rearrange("p (c u) -> p c u", u=2)

        def bank_values(j):
            return slice(j * BANK_VALUES, (j + 1) * BANK_VALUES)

        x_codes = const.tile([P, HEAD_VECTORS], U32, align_bytes=64)
        x_scales = const.tile([P, HEAD_VECTORS], U8, align_bytes=64)
        with tc.tile_pool(name="x_stage", bufs=1) as x_stage:
            x_natural = x_stage.tile([P, TOKEN_BLOCKS * FEATURES], BF16)
            x_blocks = x_natural[:].rearrange("p (k d) -> p k d", d=FEATURES)
            for block in range(TOKEN_BLOCKS):
                for partition, row, count in block_rows(block):
                    nc.sync.dma_start(
                        out=x_blocks[partition : partition + count, block, :],
                        in_=x_rows[row : row + count, :],
                    )
            x_words = x_natural[:].bitcast(F32).rearrange(
                "p (j r u q) -> p j u r q", r=2, u=2, q=P
            )
            x_grouped = x_stage.tile([P, PACK * HEAD_VECTORS], BF16, align_bytes=64)
            for j in range(HEAD_VECTORS // BANK_COLUMNS):
                bank = transposed_bank(x_words[:, j], "raw0")
                nc.vector.tensor_copy(out=like_bank(x_grouped[:, bank_values(j)]), in_=bank)
            nc.vector.quantize_mx(
                out=x_codes[:].bitcast(FP8X4), scales=x_scales[:], in_=x_grouped[:]
            )

        h_codes = const.tile([P, PAIRS * UNITS * P], U32, align_bytes=64)
        h_scales = const.tile([P, PAIRS * UNITS * P], U8, align_bytes=64)

        def h_slot(pair, unit, low, high):
            first = (pair * UNITS + unit) * P
            return slice(first + low, first + high)

        for pair in range(GROUPS, PAIRS):
            other_low = GROUP_ROWS - token_columns(pair)[0]
            all_units = h_slot(pair, 0, 0, UNITS * P)
            nc.vector.memset(
                h_codes[:, all_units]
                .bitcast(I32)
                .rearrange("p (n k) -> p n k", k=P)[:, :, other_low : other_low + GROUP_ROWS],
                0,
            )
            nc.vector.memset(
                h_scales[:, all_units]
                .bitcast(I32)
                .rearrange("p (n k) -> p n k", k=P // 4)[
                    :, :, other_low // 4 : (other_low + GROUP_ROWS) // 4
                ],
                0,
            )

        def load_first(unit):
            loaded = natural.tile([P, EXPERTS * UNIT_VALUES], BF16, name="loaded", tag="loaded")
            by_expert = loaded[:].rearrange("p (e r v) -> p e r v", e=EXPERTS, r=2)
            rows = slice(unit * K_PASS, (unit + 1) * K_PASS)
            for e in range(EXPERTS):
                nc.sync.dma_start(
                    out=by_expert[:, e],
                    in_=first_linear[e, rows, :].rearrange("(r p j) d -> p r (j d)", p=P, j=2),
                )
            return loaded[:].bitcast(F32).rearrange(
                "p (e r j u q) -> p e j u r q", e=EXPERTS, r=2, j=2, u=2
            )

        def load_second(unit):
            loaded = natural.tile([P, EXPERTS * UNIT_VALUES], BF16, name="loaded", tag="loaded")
            columns = slice(unit * K_PASS, (unit + 1) * K_PASS)
            nc.sync.dma_start(
                out=loaded[:].rearrange("p (b i) -> p b i", i=K_PASS),
                in_=second_linear[:, :, columns].rearrange("e (b p) i -> p (e b) i", p=P),
            )
            return loaded[:].bitcast(F32).rearrange(
                "p (e j r u q) -> p e j u r q", e=EXPERTS, j=2, r=2, u=2
            )

        def merged_unit(words):
            grouped = work.tile([P, PAIRS, UNIT_VALUES], BF16, align_bytes=64)
            for j in range(UNIT_BANKS):
                raw = [transposed_bank(words[:, e, j], "raw%d" % e) for e in range(EXPERTS)]
                for pair in range(PAIRS):
                    scaled = work.tile([P, BANK_VALUES], F32, bufs=4)
                    nc.scalar.activation(
                        out=like_bank(scaled[:]),
                        in_=raw[1],
                        func=COPY,
                        scale=mixing_weight(pair, 1),
                    )
                    nc.vector.scalar_tensor_tensor(
                        out=like_bank(grouped[:, pair, bank_values(j)]),
                        in0=raw[0],
                        scalar=mixing_weight(pair, 0),
                        in1=like_bank(scaled[:]),
                        op0=MULT,
                        op1=ADD,
                    )
            codes = work.tile([P, PAIRS, UNIT_WORDS], U32, align_bytes=64)
            scales = work.tile([P, PAIRS, UNIT_WORDS], U8, align_bytes=64)
            for pair in range(PAIRS):
                nc.vector.quantize_mx(
                    out=codes[:, pair, :].bitcast(FP8X4),
                    scales=scales[:, pair, :],
                    in_=grouped[:, pair, :],
                )
            return codes, scales

        with tc.psum_pool(name="hidden_psum", bufs=2) as hidden_psum:
            for unit in range(UNITS):
                codes, scales = merged_unit(load_first(unit))
                for pair in range(PAIRS):
                    tokens = slice(token_block(pair) * P, (token_block(pair) + 1) * P)
                    h_psum = hidden_psum.tile([P, PACK, P], F32)
                    for t in range(PACK):
                        hidden_units = slice(t * P, (t + 1) * P)
                        nc.tensor.matmul_mx(
                            out=h_psum[:, t, :],
                            lhsT=codes[:, pair, hidden_units].bitcast(FP8X4),
                            lhsT_scale=scales[:, pair, hidden_units],
                            rhs=x_codes[:, tokens].bitcast(FP8X4),
                            rhs_scale=x_scales[:, tokens],
                            start=True,
                            stop=True,
                        )
                    low, high = token_columns(pair)
                    values = (high - low) * PACK
                    h_grouped = work.tile([P, P * PACK], BF16, bufs=4, align_bytes=64)
                    nc.scalar.activation(
                        out=h_grouped[:, :values].rearrange("p (k t) -> p k t", t=PACK),
                        in_=h_psum[:, :, low:high].rearrange("p t k -> p k t"),
                        func=RELU,
                    )
                    slot = h_slot(pair, unit, low, high)
                    nc.vector.quantize_mx(
                        out=h_codes[:, slot].bitcast(FP8X4),
                        scales=h_scales[:, slot],
                        in_=h_grouped[:, :values],
                    )

        with tc.psum_pool(name="out_psum", bufs=1) as out_psum:
            sums = [
                out_psum.tile([P, FEATURES], F32, name="sum%d" % block)
                for block in range(TOKEN_BLOCKS)
            ]
            for unit in range(UNITS):
                codes, scales = merged_unit(load_second(unit))
                for pair in range(PAIRS):
                    low, high = token_columns(pair)
                    slot = h_slot(pair, unit, 0, P)
                    nc.tensor.matmul_mx(
                        out=sums[token_block(pair)][:],
                        lhsT=h_codes[:, slot].bitcast(FP8X4),
                        lhsT_scale=h_scales[:, slot],
                        rhs=codes[:, pair, :].bitcast(FP8X4),
                        rhs_scale=scales[:, pair, :],
                        start=unit == 0 and low == 0,
                        stop=unit == UNITS - 1 and high == P,
                    )

            for block in range(TOKEN_BLOCKS):
                result = work.tile([P, FEATURES], F32)
                nc.scalar.copy(out=result[:], in_=sums[block][:])
                for partition, row, count in block_rows(block):
                    nc.sync.dma_start(
                        out=out_rows[row : row + count, :],
                        in_=result[partition : partition + count, :],
                    )
